import numpy as np
import ml_dtypes


def mxq(x, axis, fmt="e4m3"):
    dtype, down = {"e4m3": (ml_dtypes.float8_e4m3fn, 7), "e5m2": (ml_dtypes.float8_e5m2, 14)}[fmt]
    v = np.moveaxis(np.asarray(x, np.float32).astype(ml_dtypes.bfloat16).astype(np.float64), axis, -1)
    blocks = v.reshape(v.shape[:-1] + (-1, 32))
    amax = np.abs(blocks).max(-1, keepdims=True)
    byte = np.maximum(np.where(amax > 0, np.frexp(amax)[1] - 1 + 127, 0) - down, 1)
    scale = np.exp2(byte - 127.0)
    codes = (blocks / scale).astype(np.float32).astype(dtype).astype(np.float64)
    return np.moveaxis((codes * scale).reshape(v.shape), -1, axis)


WIDE = False


def mx_kscale(k):
    if not WIDE:
        return np.ones(k)
    levels = np.array([10, -10, 5, -5, 0])
    a = np.random.permutation(np.resize(levels, k // 512 * 4)).reshape(k // 512, 4)
    idx = np.arange(k)
    return np.exp2(a[idx // 512, idx % 128 // 32])


BF16 = ml_dtypes.bfloat16


def bf(x):
    return np.asarray(x, np.float32).astype(BF16)


def f64(x):
    return np.asarray(x).astype(np.float64)


E2M1 = np.array([0.0, 0.5, 1.0, 1.5, 2.0, 3.0, 4.0, 6.0, -0.0, -0.5, -1.0, -1.5, -2.0, -3.0, -4.0, -6.0])


def pack_weight(w, fmt):
    k, n = w.shape
    w = f64(bf(w)).reshape(k // 32, 32, n)
    amax = np.abs(w).max(1)
    if fmt == "e4m3":
        byte = np.frexp(amax)[1] - 1 + 127 - 7
    else:
        mant, ex = np.frexp(amax / 6.0)
        byte = np.where(mant > 0.5, ex, ex - 1) + 127
    byte = np.clip(np.where(amax > 0, byte, 1), 1, 254)
    scaled = (w * np.exp2(127.0 - byte)[:, None, :]).reshape(k, n).astype(np.float32)
    by_word = np.ascontiguousarray(scaled.reshape(k // 512, 128, 4, n).transpose(0, 1, 3, 2))
    if fmt == "e4m3":
        words = by_word.astype(ml_dtypes.float8_e4m3fn).view(np.uint8)
    else:
        c = by_word.astype(ml_dtypes.float4_e2m1fn).view(np.uint8) & 0xF
        words = c[..., 0::2] | (c[..., 1::2] << 4)
    return np.ascontiguousarray(words), np.ascontiguousarray(byte.astype(np.uint8).reshape(k // 512, 16, n))


def unpack_weight(words, scales, fmt):
    g, p, n, _ = words.shape
    if fmt == "e4m3":
        vals = np.ascontiguousarray(words).view(ml_dtypes.float8_e4m3fn).astype(np.float64)
    else:
        nib = np.empty((g, p, n, 4), np.uint8)
        nib[..., 0::2] = words & 0xF
        nib[..., 1::2] = words >> 4
        vals = E2M1[nib]
    vals = vals * np.repeat(np.exp2(scales.astype(np.float64) - 127.0), 8, axis=1)[..., None]
    return vals.transpose(0, 1, 3, 2).reshape(g * 512, n)

def pack4(w):
    words, scales = pack_weight(w, "e2m1")
    return words.reshape(words.shape[0], 128, -1), scales


def unpack4(words, scales):
    return unpack_weight(words.reshape(words.shape[0], 128, -1, 2), scales, "e2m1")


T, K, E, H, KVH, D = 8192, 1024, 1024, 2, 4, 64
EPS = 1e-05


def rmsnorm(x, w):
    var = np.mean(np.square(x), axis=-1, keepdims=True)
    return x * (1.0 / np.sqrt(var + EPS)) * w


def setup_inputs():
    s = mx_kscale(E)
    hidden_states = bf(np.random.standard_normal((T, E)) * s)
    wq = np.random.standard_normal((H * D, E)) / np.sqrt(E) / s
    words, scales = pack4(np.ascontiguousarray(wq.T))
    q_norm_w = bf(1.5 + 0.1 * np.random.standard_normal(D))
    return {"hidden_states": hidden_states,
            "Wq_words": words,
            "Wq_scales": scales,
            "q_norm_w": q_norm_w}


def reference(hidden_states, Wq_words, Wq_scales, q_norm_w):
    q = mxq(f64(hidden_states), 1, "e4m3") @ unpack4(Wq_words, Wq_scales)
    qh = rmsnorm(q.reshape(T, H, D), f64(q_norm_w))
    return qh.transpose(1, 0, 2)

@@ -1,0 +1,170 @@
+from contextlib import ExitStack
+
+import concourse.mybir as mybir
+from concourse.masks import make_identity
+
+BF16 = mybir.dt.bfloat16
+F32 = mybir.dt.float32
+I32 = mybir.dt.int32
+U8 = mybir.dt.uint8
+U32 = mybir.dt.uint32
+FP8X4 = mybir.dt.float8_e4m3fn_x4
+FP4X4 = mybir.dt.float4_e2m1fn_x4
+ACT = mybir.ActivationFunctionType
+ALU = mybir.AluOpType
+
+P = 128
+T, E = 8192, 1024
+HEADS, D = 2, 64
+N = HEADS * D
+EPS = 1e-05
+K_PASS = 4 * P
+PASSES = E // K_PASS
+TILES = T // P
+ROUND = 4
+ROUNDS = TILES // ROUND
+HALVES = 2
+XT_BANKS = 6
+
+FLOPS = 2 * T * E * N
+
+
+def tile_combcrossattention_pa_t_kernel(tc, hidden_states, Wq_words, Wq_scales, q_norm_w, out):
+    nc = tc.nc
+    x_view = hidden_states.rearrange("(p i) k -> p (i k)", p=P)
+    out_view = out.rearrange("h (p i) d -> p h i d", p=P)
+
+    with ExitStack() as ctx:
+        const = ctx.enter_context(tc.tile_pool(name="const", bufs=1))
+        x_pool = ctx.enter_context(tc.tile_pool(name="x", bufs=ROUNDS))
+        work = ctx.enter_context(tc.tile_pool(name="work", bufs=3))
+        o_pool = ctx.enter_context(tc.tile_pool(name="o", bufs=ROUNDS))
+        xt_pool = ctx.enter_context(tc.psum_pool(name="xt", bufs=XT_BANKS))
+        q_pool = ctx.enter_context(tc.psum_pool(name="q", bufs=2))
+        ctx.enter_context(tc.manual_schedule())
+
+        w_planes = const.tile([P, PASSES, N], U8, align_bytes=64)
+        nc.vector.memset(w_planes[:].bitcast(I32), 0)
+        eps = const.tile([P, 1], F32)
+        nc.vector.memset(eps[:], EPS)
+        warm = const.tile([P, 1], F32)
+        nc.scalar.activation(out=warm[:], in_=eps[:], func=ACT.Sqrt)
+        ident = const.tile([P, P], F32)
+        make_identity(nc, ident[:])
+
+        x_sb = []
+        for r in range(ROUNDS):
+            x_chunk = x_pool.tile([P, ROUND * E], BF16)
+            x_sb.append(x_chunk)
+
+        def load_x(r):
+            nc.sync.dma_start(out=x_sb[r][:], in_=x_view[:, r * ROUND * E : (r + 1) * ROUND * E])
+
+        load_x(0)
+        w_words = const.tile([P, PASSES, 2 * N], U8, align_bytes=64)
+        nc.sync.dma_start(out=w_words[:].bitcast(I32), in_=Wq_words.rearrange("g p b -> p g b").bitcast(I32))
+        for quad in range(4):
+            nc.sync.dma_start(
+                out=w_planes[32 * quad : 32 * quad + 4].bitcast(I32),
+                in_=Wq_scales[:, 4 * quad : 4 * quad + 4, :].rearrange("g s n -> s g n").bitcast(I32),
+            )
+        gain_bf = const.tile([P, D], BF16)
+        nc.scalar.dma_start(out=gain_bf[:], in_=q_norm_w.partition_broadcast(P))
+        gain = const.tile([P, D], F32)
+        nc.vector.tensor_copy(out=gain[:], in_=gain_bf[:])
+        for r in range(1, ROUNDS):
+            load_x(r)
+
+        grouped_of, codes_of, scales_of, q_of = {}, {}, {}, {}
+
+        def transpose_and_copy(r):
+            x_words = x_sb[r][:].bitcast(F32)
+            grouped = work.tile([P, ROUND, PASSES, P, 4], BF16, align_bytes=64)
+            grouped_of[r] = grouped
+            banks = []
+            for i in range(ROUND):
+                xt = xt_pool.tile([P, PASSES * HALVES, P], F32)
+                banks.append(xt)
+                for g in range(PASSES):
+                    for u in range(HALVES):
+                        first = (i * PASSES + g) * (K_PASS // 2)
+                        nc.tensor.transpose(
+                            xt[:, g * HALVES + u, :],
+                            x_words[:, first + u : first + K_PASS // 2 : HALVES],
+                            ident[:],
+                        )
+            for i in range(ROUND):
+                src = banks[i][:].rearrange("p (g u) c -> p g c u", u=HALVES)
+                dst = grouped[:, i].bitcast(F32)
+                if i == 0:
+                    nc.vector.tensor_copy(out=dst, in_=src)
+                else:
+                    nc.scalar.copy(out=dst, in_=src)
+
+        def quantise(r):
+            codes = work.tile([P, ROUND * PASSES * P], U32, align_bytes=64)
+            x_scales = work.tile([P, ROUND * PASSES * P], U8, align_bytes=64)
+            codes_of[r], scales_of[r] = codes, x_scales
+            nc.vector.quantize_mx(
+                out=codes[:].bitcast(FP8X4),
+                scales=x_scales[:],
+                in_=grouped_of[r][:].rearrange("p i g c t -> p (i g c t)"),
+            )
+
+        def multiply(r):
+            q_ps = q_pool.tile([P, ROUND, N], F32)
+            q_of[r] = q_ps
+            for i in range(ROUND):
+                for g in range(PASSES):
+                    cols = slice((i * PASSES + g) * P, (i * PASSES + g + 1) * P)
+                    nc.tensor.matmul_mx(
+                        out=q_ps[:, i, :],
+                        lhsT=codes_of[r][:, cols].bitcast(FP8X4),
+                        lhsT_scale=scales_of[r][:, cols],
+                        rhs=w_words[:, g, :].bitcast(FP4X4),
+                        rhs_scale=w_planes[:, g, :],
+                        start=(g == 0),
+                        stop=(g == PASSES - 1),
+                    )
+
+        def norm_and_store(r):
+            q_ps = q_of[r]
+            squares = work.tile([P, ROUND * HEADS, D], F32)
+            mean_sq = work.tile([P, ROUND * HEADS], F32)
+            for i in range(ROUND):
+                for h in range(HEADS):
+                    c = i * HEADS + h
+                    nc.scalar.activation(
+                        out=squares[:, c, :],
+                        in_=q_ps[:, i, h * D : (h + 1) * D],
+                        func=ACT.Square,
+                        scale=D ** -0.5,
+                        accum_out=mean_sq[:, c : c + 1],
+                    )
+            rms = work.tile([P, ROUND * HEADS], F32)
+            nc.scalar.activation(out=rms[:], in_=mean_sq[:], func=ACT.Sqrt, bias=eps[:, 0:1])
+            rstd = work.tile([P, ROUND * HEADS], F32)
+            nc.vector.reciprocal(out=rstd[:], in_=rms[:])
+            o_sb = o_pool.tile([P, HEADS, ROUND, D], F32)
+            for i in range(ROUND):
+                for h in range(HEADS):
+                    c = i * HEADS + h
+                    nc.vector.scalar_tensor_tensor(
+                        out=o_sb[:, h, i, :],
+                        in0=q_ps[:, i, h * D : (h + 1) * D],
+                        scalar=rstd[:, c : c + 1],
+                        in1=gain[:],
+                        op0=ALU.mult,
+                        op1=ALU.mult,
+                    )
+            nc.sync.dma_start(out=out_view[:, :, r * ROUND : (r + 1) * ROUND, :], in_=o_sb[:])
+
+        for r in range(ROUNDS + 2):
+            if 1 <= r <= ROUNDS:
+                quantise(r - 1)
+            if r >= 2:
+                norm_and_store(r - 2)
+            if r < ROUNDS:
+                transpose_and_copy(r)
+            if 1 <= r <= ROUNDS:
+                multiply(r - 1)

@@ -23,8 +23,10 @@ PASSES = E // K_PASS
 TILES = T // P
 ROUND = 4
 ROUNDS = TILES // ROUND
+STRETCH = 4
+STRETCHES = ROUNDS // STRETCH
 HALVES = 2
-XT_BANKS = 6
+XT_BANKS = 8 - STRETCH
 
 FLOPS = 2 * T * E * N
 
@@ -38,9 +40,10 @@ def tile_combcrossattention_pa_t_kernel(tc, hidden_states, Wq_words, Wq_scales, 
         const = ctx.enter_context(tc.tile_pool(name="const", bufs=1))
         x_pool = ctx.enter_context(tc.tile_pool(name="x", bufs=ROUNDS))
         work = ctx.enter_context(tc.tile_pool(name="work", bufs=3))
+        mx_pool = ctx.enter_context(tc.tile_pool(name="mx", bufs=STRETCH))
         o_pool = ctx.enter_context(tc.tile_pool(name="o", bufs=ROUNDS))
         xt_pool = ctx.enter_context(tc.psum_pool(name="xt", bufs=XT_BANKS))
-        q_pool = ctx.enter_context(tc.psum_pool(name="q", bufs=2))
+        q_pool = ctx.enter_context(tc.psum_pool(name="q", bufs=STRETCH))
         ctx.enter_context(tc.manual_schedule())
 
         w_planes = const.tile([P, PASSES, N], U8, align_bytes=64)
@@ -52,15 +55,24 @@ def tile_combcrossattention_pa_t_kernel(tc, hidden_states, Wq_words, Wq_scales, 
         ident = const.tile([P, P], F32)
         make_identity(nc, ident[:])
 
+        gain = const.tile([P, D], BF16)
+        nc.scalar.dma_start(out=gain[:], in_=q_norm_w.partition_broadcast(P))
         x_sb = []
         for r in range(ROUNDS):
             x_chunk = x_pool.tile([P, ROUND * E], BF16)
             x_sb.append(x_chunk)
 
-        def load_x(r):
-            nc.sync.dma_start(out=x_sb[r][:], in_=x_view[:, r * ROUND * E : (r + 1) * ROUND * E])
+        def load_x(r, pieces):
+            width = ROUND * E // pieces
+            for c in range(pieces):
+                nc.sync.dma_start(
+                    out=x_sb[r][:, c * width : (c + 1) * width],
+                    in_=x_view[:, r * ROUND * E + c * width : r * ROUND * E + (c + 1) * width],
+                )
 
-        load_x(0)
+        load_x(0, ROUND)
+        for r in range(1, STRETCH):
+            load_x(r, 1)
         w_words = const.tile([P, PASSES, 2 * N], U8, align_bytes=64)
         nc.sync.dma_start(out=w_words[:].bitcast(I32), in_=Wq_words.rearrange("g p b -> p g b").bitcast(I32))
         for quad in range(4):
@@ -68,12 +80,8 @@ def tile_combcrossattention_pa_t_kernel(tc, hidden_states, Wq_words, Wq_scales, 
                 out=w_planes[32 * quad : 32 * quad + 4].bitcast(I32),
                 in_=Wq_scales[:, 4 * quad : 4 * quad + 4, :].rearrange("g s n -> s g n").bitcast(I32),
             )
-        gain_bf = const.tile([P, D], BF16)
-        nc.scalar.dma_start(out=gain_bf[:], in_=q_norm_w.partition_broadcast(P))
-        gain = const.tile([P, D], F32)
-        nc.vector.tensor_copy(out=gain[:], in_=gain_bf[:])
-        for r in range(1, ROUNDS):
-            load_x(r)
+        for r in range(STRETCH, ROUNDS):
+            load_x(r, 1)
 
         grouped_of, codes_of, scales_of, q_of = {}, {}, {}, {}
 
@@ -96,20 +104,23 @@ def tile_combcrossattention_pa_t_kernel(tc, hidden_states, Wq_words, Wq_scales, 
             for i in range(ROUND):
                 src = banks[i][:].rearrange("p (g u) c -> p g c u", u=HALVES)
                 dst = grouped[:, i].bitcast(F32)
-                if i == 0:
+                if i == ROUND - 1:
                     nc.vector.tensor_copy(out=dst, in_=src)
                 else:
                     nc.scalar.copy(out=dst, in_=src)
 
         def quantise(r):
-            codes = work.tile([P, ROUND * PASSES * P], U32, align_bytes=64)
-            x_scales = work.tile([P, ROUND * PASSES * P], U8, align_bytes=64)
+            codes = mx_pool.tile([P, ROUND * PASSES * P], U32, align_bytes=64)
+            x_scales = mx_pool.tile([P, ROUND * PASSES * P], U8, align_bytes=64)
             codes_of[r], scales_of[r] = codes, x_scales
-            nc.vector.quantize_mx(
-                out=codes[:].bitcast(FP8X4),
-                scales=x_scales[:],
-                in_=grouped_of[r][:].rearrange("p i g c t -> p (i g c t)"),
-            )
+            pair = ROUND // 2
+            for c in range(2):
+                cols = slice(c * pair * PASSES * P, (c + 1) * pair * PASSES * P)
+                nc.vector.quantize_mx(
+                    out=codes[:, cols].bitcast(FP8X4),
+                    scales=x_scales[:, cols],
+                    in_=grouped_of[r][:, c * pair : (c + 1) * pair].rearrange("p i g c t -> p (i g c t)"),
+                )
 
         def multiply(r):
             q_ps = q_pool.tile([P, ROUND, N], F32)
@@ -159,12 +170,13 @@ def tile_combcrossattention_pa_t_kernel(tc, hidden_states, Wq_words, Wq_scales, 
                     )
             nc.sync.dma_start(out=out_view[:, :, r * ROUND : (r + 1) * ROUND, :], in_=o_sb[:])
 
-        for r in range(ROUNDS + 2):
-            if 1 <= r <= ROUNDS:
-                quantise(r - 1)
-            if r >= 2:
-                norm_and_store(r - 2)
-            if r < ROUNDS:
-                transpose_and_copy(r)
-            if 1 <= r <= ROUNDS:
-                multiply(r - 1)
+        for s in range(STRETCHES + 1):
+            if s > 0:
+                for r in range((s - 1) * STRETCH, s * STRETCH):
+                    norm_and_store(r)
+            if s < STRETCHES:
+                for r in range(s * STRETCH, (s + 1) * STRETCH):
+                    transpose_and_copy(r)
+                    quantise(r)
+                for r in range(s * STRETCH, (s + 1) * STRETCH):
+                    multiply(r)

@@ -23,27 +23,24 @@ PASSES = E // K_PASS
 TILES = T // P
 ROUND = 4
 ROUNDS = TILES // ROUND
-STRETCH = 4
-STRETCHES = ROUNDS // STRETCH
 HALVES = 2
-XT_BANKS = 8 - STRETCH
+XT_BANKS = 6
 
 FLOPS = 2 * T * E * N
 
 
 def tile_combcrossattention_pa_t_kernel(tc, hidden_states, Wq_words, Wq_scales, q_norm_w, out):
     nc = tc.nc
-    x_view = hidden_states.rearrange("(p i) k -> p (i k)", p=P)
-    out_view = out.rearrange("h (p i) d -> p h i d", p=P)
+    x_view = hidden_states.rearrange("(r p i) k -> r p (i k)", p=P, i=ROUND)
+    out_view = out.rearrange("h (r p i) d -> r p h (i d)", p=P, i=ROUND)
 
     with ExitStack() as ctx:
         const = ctx.enter_context(tc.tile_pool(name="const", bufs=1))
         x_pool = ctx.enter_context(tc.tile_pool(name="x", bufs=ROUNDS))
         work = ctx.enter_context(tc.tile_pool(name="work", bufs=3))
-        mx_pool = ctx.enter_context(tc.tile_pool(name="mx", bufs=STRETCH))
         o_pool = ctx.enter_context(tc.tile_pool(name="o", bufs=ROUNDS))
         xt_pool = ctx.enter_context(tc.psum_pool(name="xt", bufs=XT_BANKS))
-        q_pool = ctx.enter_context(tc.psum_pool(name="q", bufs=STRETCH))
+        q_pool = ctx.enter_context(tc.psum_pool(name="q", bufs=2))
         ctx.enter_context(tc.manual_schedule())
 
         w_planes = const.tile([P, PASSES, N], U8, align_bytes=64)
@@ -65,14 +62,10 @@ def tile_combcrossattention_pa_t_kernel(tc, hidden_states, Wq_words, Wq_scales, 
         def load_x(r, pieces):
             width = ROUND * E // pieces
             for c in range(pieces):
-                nc.sync.dma_start(
-                    out=x_sb[r][:, c * width : (c + 1) * width],
-                    in_=x_view[:, r * ROUND * E + c * width : r * ROUND * E + (c + 1) * width],
-                )
+                cols = slice(c * width, (c + 1) * width)
+                nc.sync.dma_start(out=x_sb[r][:, cols], in_=x_view[r][:, cols])
 
         load_x(0, ROUND)
-        for r in range(1, STRETCH):
-            load_x(r, 1)
         w_words = const.tile([P, PASSES, 2 * N], U8, align_bytes=64)
         nc.sync.dma_start(out=w_words[:].bitcast(I32), in_=Wq_words.rearrange("g p b -> p g b").bitcast(I32))
         for quad in range(4):
@@ -80,7 +73,7 @@ def tile_combcrossattention_pa_t_kernel(tc, hidden_states, Wq_words, Wq_scales, 
                 out=w_planes[32 * quad : 32 * quad + 4].bitcast(I32),
                 in_=Wq_scales[:, 4 * quad : 4 * quad + 4, :].rearrange("g s n -> s g n").bitcast(I32),
             )
-        for r in range(STRETCH, ROUNDS):
+        for r in range(1, ROUNDS):
             load_x(r, 1)
 
         grouped_of, codes_of, scales_of, q_of = {}, {}, {}, {}
@@ -104,23 +97,20 @@ def tile_combcrossattention_pa_t_kernel(tc, hidden_states, Wq_words, Wq_scales, 
             for i in range(ROUND):
                 src = banks[i][:].rearrange("p (g u) c -> p g c u", u=HALVES)
                 dst = grouped[:, i].bitcast(F32)
-                if i == ROUND - 1:
+                if i == 0:
                     nc.vector.tensor_copy(out=dst, in_=src)
                 else:
                     nc.scalar.copy(out=dst, in_=src)
 
         def quantise(r):
-            codes = mx_pool.tile([P, ROUND * PASSES * P], U32, align_bytes=64)
-            x_scales = mx_pool.tile([P, ROUND * PASSES * P], U8, align_bytes=64)
+            codes = work.tile([P, ROUND * PASSES * P], U32, align_bytes=64)
+            x_scales = work.tile([P, ROUND * PASSES * P], U8, align_bytes=64)
             codes_of[r], scales_of[r] = codes, x_scales
-            pair = ROUND // 2
-            for c in range(2):
-                cols = slice(c * pair * PASSES * P, (c + 1) * pair * PASSES * P)
-                nc.vector.quantize_mx(
-                    out=codes[:, cols].bitcast(FP8X4),
-                    scales=x_scales[:, cols],
-                    in_=grouped_of[r][:, c * pair : (c + 1) * pair].rearrange("p i g c t -> p (i g c t)"),
-                )
+            nc.vector.quantize_mx(
+                out=codes[:].bitcast(FP8X4),
+                scales=x_scales[:],
+                in_=grouped_of[r][:].rearrange("p i g c t -> p (i g c t)"),
+            )
 
         def multiply(r):
             q_ps = q_pool.tile([P, ROUND, N], F32)
@@ -168,15 +158,14 @@ def tile_combcrossattention_pa_t_kernel(tc, hidden_states, Wq_words, Wq_scales, 
                         op0=ALU.mult,
                         op1=ALU.mult,
                     )
-            nc.sync.dma_start(out=out_view[:, :, r * ROUND : (r + 1) * ROUND, :], in_=o_sb[:])
+            nc.sync.dma_start(out=out_view[r], in_=o_sb[:].rearrange("p h i d -> p h (i d)"))
 
-        for s in range(STRETCHES + 1):
-            if s > 0:
-                for r in range((s - 1) * STRETCH, s * STRETCH):
-                    norm_and_store(r)
-            if s < STRETCHES:
-                for r in range(s * STRETCH, (s + 1) * STRETCH):
-                    transpose_and_copy(r)
-                    quantise(r)
-                for r in range(s * STRETCH, (s + 1) * STRETCH):
-                    multiply(r)
+        for r in range(ROUNDS + 2):
+            if 1 <= r <= ROUNDS:
+                quantise(r - 1)
+            if r >= 2:
+                norm_and_store(r - 2)
+            if r < ROUNDS:
+                transpose_and_copy(r)
+            if 1 <= r <= ROUNDS:
+                multiply(r - 1)

@@ -41,7 +41,6 @@ def tile_combcrossattention_pa_t_kernel(tc, hidden_states, Wq_words, Wq_scales, 
         o_pool = ctx.enter_context(tc.tile_pool(name="o", bufs=ROUNDS))
         xt_pool = ctx.enter_context(tc.psum_pool(name="xt", bufs=XT_BANKS))
         q_pool = ctx.enter_context(tc.psum_pool(name="q", bufs=2))
-        ctx.enter_context(tc.manual_schedule())
 
         w_planes = const.tile([P, PASSES, N], U8, align_bytes=64)
         nc.vector.memset(w_planes[:].bitcast(I32), 0)

@@ -24,6 +24,7 @@ TILES = T // P
 ROUND = 4
 ROUNDS = TILES // ROUND
 HALVES = 2
+FINE_ROUNDS = 3
 XT_BANKS = 6
 
 FLOPS = 2 * T * E * N
@@ -73,7 +74,7 @@ def tile_combcrossattention_pa_t_kernel(tc, hidden_states, Wq_words, Wq_scales, 
                 in_=Wq_scales[:, 4 * quad : 4 * quad + 4, :].rearrange("g s n -> s g n").bitcast(I32),
             )
         for r in range(1, ROUNDS):
-            load_x(r, 1)
+            load_x(r, ROUND if r < FINE_ROUNDS else 1)
 
         grouped_of, codes_of, scales_of, q_of = {}, {}, {}, {}
 

@@ -26,6 +26,21 @@ ROUNDS = TILES // ROUND
 HALVES = 2
 FINE_ROUNDS = 3
 XT_BANKS = 6
+V_EXTRA_EVERY = 0
+V_SKIP_EVERY = 0
+TAIL_UNITS = [2, 1, 1]
+Q_UNITS = [4]
+GAIN_BY_PE = False
+WARM = 0
+RSQRT = True
+G_GAIN = False
+WIDE_SQ = False
+G_PIECES = 1
+G_NOT_LAST = 2
+SPLIT_LAST = False
+G_SCALE = False
+PRE_TILES = ()
+PRE_FROM = 3
 
 FLOPS = 2 * T * E * N
 
@@ -39,21 +54,40 @@ def tile_combcrossattention_pa_t_kernel(tc, hidden_states, Wq_words, Wq_scales, 
         const = ctx.enter_context(tc.tile_pool(name="const", bufs=1))
         x_pool = ctx.enter_context(tc.tile_pool(name="x", bufs=ROUNDS))
         work = ctx.enter_context(tc.tile_pool(name="work", bufs=3))
-        o_pool = ctx.enter_context(tc.tile_pool(name="o", bufs=ROUNDS))
+        o_pool = ctx.enter_context(tc.tile_pool(name="o", bufs=ROUNDS + len(TAIL_UNITS)))
         xt_pool = ctx.enter_context(tc.psum_pool(name="xt", bufs=XT_BANKS))
         q_pool = ctx.enter_context(tc.psum_pool(name="q", bufs=2))
+        pre_pool = ctx.enter_context(tc.tile_pool(name="pre", bufs=4))
 
         w_planes = const.tile([P, PASSES, N], U8, align_bytes=64)
         nc.vector.memset(w_planes[:].bitcast(I32), 0)
         eps = const.tile([P, 1], F32)
         nc.vector.memset(eps[:], EPS)
         warm = const.tile([P, 1], F32)
-        nc.scalar.activation(out=warm[:], in_=eps[:], func=ACT.Sqrt)
+        nc.scalar.activation(out=warm[:], in_=eps[:], func=(ACT.Abs_reciprocal_sqrt if RSQRT else ACT.Sqrt))
         ident = const.tile([P, P], F32)
         make_identity(nc, ident[:])
 
         gain = const.tile([P, D], BF16)
-        nc.scalar.dma_start(out=gain[:], in_=q_norm_w.partition_broadcast(P))
+        if GAIN_BY_PE or WARM:
+            ones = const.tile([P, P], BF16)
+            nc.vector.memset(ones[:], 1.0)
+        if WARM:
+            dummy = const.tile([P, 4 * P], BF16)
+            nc.vector.memset(dummy[:], 0.0)
+            for w in range(WARM):
+                xt = xt_pool.tile([P, PASSES * HALVES, P], F32)
+                nc.tensor.matmul(xt[:].rearrange("p a b -> p (a b)"), lhsT=ones[:], rhs=dummy[:], start=True, stop=True)
+        if GAIN_BY_PE:
+            gain_row = const.tile([P, D], BF16)
+            nc.vector.memset(gain_row[:], 0.0)
+            nc.scalar.dma_start(out=gain_row[0:1, :], in_=q_norm_w.rearrange("(o d) -> o d", o=1))
+        else:
+            nc.scalar.dma_start(out=gain[:], in_=q_norm_w.partition_broadcast(P))
+        if G_SCALE or G_GAIN:
+            gain_all = const.tile([P, ROUND * HEADS, D], BF16)
+            for c in range(ROUND * HEADS):
+                nc.gpsimd.tensor_copy(out=gain_all[:, c, :], in_=gain[:])
         x_sb = []
         for r in range(ROUNDS):
             x_chunk = x_pool.tile([P, ROUND * E], BF16)
@@ -76,48 +110,76 @@ def tile_combcrossattention_pa_t_kernel(tc, hidden_states, Wq_words, Wq_scales, 
         for r in range(1, ROUNDS):
             load_x(r, ROUND if r < FINE_ROUNDS else 1)
 
-        grouped_of, codes_of, scales_of, q_of = {}, {}, {}, {}
+        if GAIN_BY_PE:
+            q_ps = q_pool.tile([P, ROUND, N], F32)
+            nc.tensor.matmul(q_ps[:, 0, 0:D], lhsT=ones[:], rhs=gain_row[:], start=True, stop=True)
+            nc.vector.tensor_copy(out=gain[:], in_=q_ps[:, 0, 0:D])
 
-        def transpose_and_copy(r):
+        grouped_of, codes_of, scales_of, q_of = {}, {}, {}, {}
+        sorted_of = {}
+
+        def sort_words(r):
+            if r < PRE_FROM or r >= ROUNDS:
+                return
             x_words = x_sb[r][:].bitcast(F32)
-            grouped = work.tile([P, ROUND, PASSES, P, 4], BF16, align_bytes=64)
-            grouped_of[r] = grouped
-            banks = []
-            for i in range(ROUND):
+            for i in PRE_TILES:
+                x_sorted = pre_pool.tile([P, PASSES, HALVES, P], F32)
+                sorted_of[(r, i)] = x_sorted
+                nc.vector.tensor_copy(
+                    out=x_sorted[:],
+                    in_=x_words[:, i * (E // 2) : (i + 1) * (E // 2)].rearrange("p (g c u) -> p g u c", g=PASSES, u=HALVES),
+                )
+
+        def transpose_and_copy(r, i0, n):
+            x_words = x_sb[r][:].bitcast(F32)
+            if i0 == 0:
+                grouped = work.tile([P, ROUND, PASSES, P, 4], BF16, align_bytes=64)
+                grouped_of[r] = grouped
+                codes = work.tile([P, ROUND * PASSES * P], U32, align_bytes=64)
+                x_scales = work.tile([P, ROUND * PASSES * P], U8, align_bytes=64)
+                codes_of[r], scales_of[r] = codes, x_scales
+            grouped = grouped_of[r]
+            banks = {}
+            for i in range(i0, i0 + n):
                 xt = xt_pool.tile([P, PASSES * HALVES, P], F32)
-                banks.append(xt)
+                banks[i] = xt
                 for g in range(PASSES):
                     for u in range(HALVES):
                         first = (i * PASSES + g) * (K_PASS // 2)
-                        nc.tensor.transpose(
-                            xt[:, g * HALVES + u, :],
-                            x_words[:, first + u : first + K_PASS // 2 : HALVES],
-                            ident[:],
-                        )
-            for i in range(ROUND):
+                        if (r, i) in sorted_of:
+                            source = sorted_of[(r, i)][:, g, u, :]
+                        else:
+                            source = x_words[:, first + u : first + K_PASS // 2 : HALVES]
+                        nc.tensor.transpose(xt[:, g * HALVES + u, :], source, ident[:])
+            v_banks = 2 if (V_EXTRA_EVERY and r % V_EXTRA_EVERY == V_EXTRA_EVERY - 1) else 1
+            if V_SKIP_EVERY and r % V_SKIP_EVERY == V_SKIP_EVERY - 1 and r < ROUNDS - G_NOT_LAST:
+                v_banks = 0
+            for i in range(i0, i0 + n):
                 src = banks[i][:].rearrange("p (g u) c -> p g c u", u=HALVES)
                 dst = grouped[:, i].bitcast(F32)
-                if i == 0:
+                if i % 2 == 0 and i // 2 < v_banks:
                     nc.vector.tensor_copy(out=dst, in_=src)
                 else:
                     nc.scalar.copy(out=dst, in_=src)
 
-        def quantise(r):
-            codes = work.tile([P, ROUND * PASSES * P], U32, align_bytes=64)
-            x_scales = work.tile([P, ROUND * PASSES * P], U8, align_bytes=64)
-            codes_of[r], scales_of[r] = codes, x_scales
+        def quantise(r, i0, n):
+            cols = slice(i0 * PASSES * P, (i0 + n) * PASSES * P)
             nc.vector.quantize_mx(
-                out=codes[:].bitcast(FP8X4),
-                scales=x_scales[:],
-                in_=grouped_of[r][:].rearrange("p i g c t -> p (i g c t)"),
+                out=codes_of[r][:, cols].bitcast(FP8X4),
+                scales=scales_of[r][:, cols],
+                in_=grouped_of[r][:, i0 : i0 + n].rearrange("p i g c t -> p (i g c t)"),
             )
 
-        def multiply(r):
-            q_ps = q_pool.tile([P, ROUND, N], F32)
-            q_of[r] = q_ps
-            for i in range(ROUND):
+        def multiply(r, i0, n):
+            if r == ROUNDS - 1 and len(TAIL_UNITS) > 1:
+                xt = xt_pool.tile([P, n, N], F32)
+                q_ps = xt
+            else:
+                q_ps = q_pool.tile([P, n, N], F32)
+            q_of[(r, i0)] = q_ps
+            for i in range(n):
                 for g in range(PASSES):
-                    cols = slice((i * PASSES + g) * P, (i * PASSES + g + 1) * P)
+                    cols = slice(((i0 + i) * PASSES + g) * P, ((i0 + i) * PASSES + g + 1) * P)
                     nc.tensor.matmul_mx(
                         out=q_ps[:, i, :],
                         lhsT=codes_of[r][:, cols].bitcast(FP8X4),
@@ -128,11 +190,28 @@ def tile_combcrossattention_pa_t_kernel(tc, hidden_states, Wq_words, Wq_scales, 
                         stop=(g == PASSES - 1),
                     )
 
-        def norm_and_store(r):
-            q_ps = q_of[r]
-            squares = work.tile([P, ROUND * HEADS, D], F32)
-            mean_sq = work.tile([P, ROUND * HEADS], F32)
-            for i in range(ROUND):
+        def norm_and_store(r, i0, n):
+            q_ps = q_of[(r, i0)]
+            if G_SCALE:
+                with_gain = work.tile([P, n * HEADS, D], F32)
+                nc.vector.tensor_tensor(
+                    out=with_gain[:],
+                    in0=q_ps[:].rearrange("p i (h d) -> p (i h) d", h=HEADS),
+                    in1=gain_all[:, 0 : n * HEADS, :],
+                    op=ALU.mult,
+                )
+            squares = work.tile([P, n * HEADS, D], F32)
+            mean_sq = work.tile([P, n * HEADS], F32)
+            wide_sq = WIDE_SQ and r < ROUNDS - G_NOT_LAST
+            if wide_sq:
+                nc.scalar.activation(
+                    out=squares[:].rearrange("p c d -> p (c d)"),
+                    in_=q_ps[:].rearrange("p i n -> p (i n)"),
+                    func=ACT.Square,
+                    scale=D ** -0.5,
+                )
+                nc.vector.tensor_reduce(out=mean_sq[:], in_=squares[:], axis=mybir.AxisListType.X, op=ALU.add)
+            for i in range(0 if wide_sq else n):
                 for h in range(HEADS):
                     c = i * HEADS + h
                     nc.scalar.activation(
@@ -142,12 +221,44 @@ def tile_combcrossattention_pa_t_kernel(tc, hidden_states, Wq_words, Wq_scales, 
                         scale=D ** -0.5,
                         accum_out=mean_sq[:, c : c + 1],
                     )
-            rms = work.tile([P, ROUND * HEADS], F32)
-            nc.scalar.activation(out=rms[:], in_=mean_sq[:], func=ACT.Sqrt, bias=eps[:, 0:1])
-            rstd = work.tile([P, ROUND * HEADS], F32)
-            nc.vector.reciprocal(out=rstd[:], in_=rms[:])
-            o_sb = o_pool.tile([P, HEADS, ROUND, D], F32)
-            for i in range(ROUND):
+            rstd = work.tile([P, n * HEADS], F32)
+            if RSQRT:
+                nc.scalar.activation(out=rstd[:], in_=mean_sq[:], func=ACT.Abs_reciprocal_sqrt, bias=eps[:, 0:1])
+            else:
+                rms = work.tile([P, n * HEADS], F32)
+                nc.scalar.activation(out=rms[:], in_=mean_sq[:], func=ACT.Sqrt, bias=eps[:, 0:1])
+                nc.vector.reciprocal(out=rstd[:], in_=rms[:])
+            o_sb = o_pool.tile([P, HEADS, n, D], F32)
+            g_path = G_GAIN and r < ROUNDS - G_NOT_LAST
+            if g_path:
+                by_rms = work.tile([P, HEADS, n, D], F32)
+                nc.vector.tensor_tensor(
+                    out=by_rms[:].rearrange("p h i d -> p i h d"),
+                    in0=q_ps[:].rearrange("p i (h d) -> p i h d", h=HEADS),
+                    in1=rstd[:].rearrange("p (i h) -> p i h", h=HEADS).unsqueeze(3).to_broadcast([P, n, HEADS, D]),
+                    op=ALU.mult,
+                )
+                rows = n * HEADS // min(G_PIECES, n * HEADS)
+                for c in range(0, n * HEADS, rows):
+                    nc.gpsimd.tensor_tensor(
+                        out=o_sb[:].rearrange("p h i d -> p (h i) d")[:, c : c + rows, :],
+                        in0=by_rms[:].rearrange("p h i d -> p (h i) d")[:, c : c + rows, :],
+                        in1=gain_all[:, c : c + rows, :],
+                        op=ALU.mult,
+                    )
+            if G_SCALE:
+                for i in range(n):
+                    for h in range(HEADS):
+                        c = i * HEADS + h
+                        nc.gpsimd.tensor_scalar(
+                            out=o_sb[:, h, i, :],
+                            in0=with_gain[:, c, :],
+                            scalar1=rstd[:, c : c + 1],
+                            scalar2=0.0,
+                            op0=ALU.mult,
+                            op1=ALU.add,
+                        )
+            for i in range(0 if (G_SCALE or g_path) else n):
                 for h in range(HEADS):
                     c = i * HEADS + h
                     nc.vector.scalar_tensor_tensor(
@@ -158,14 +269,39 @@ def tile_combcrossattention_pa_t_kernel(tc, hidden_states, Wq_words, Wq_scales, 
                         op0=ALU.mult,
                         op1=ALU.mult,
                     )
-            nc.sync.dma_start(out=out_view[r], in_=o_sb[:].rearrange("p h i d -> p h (i d)"))
+            nc.sync.dma_start(
+                out=out_view[r][:, :, i0 * D : (i0 + n) * D], in_=o_sb[:].rearrange("p h i d -> p h (i d)")
+            )
 
-        for r in range(ROUNDS + 2):
-            if 1 <= r <= ROUNDS:
-                quantise(r - 1)
+        def units(r):
+            sizes = TAIL_UNITS if r == ROUNDS - 1 else [ROUND]
+            return [(r, sum(sizes[:j]), sizes[j]) for j in range(len(sizes))]
+
+        def q_units(r):
+            sizes = TAIL_UNITS if r == ROUNDS - 1 else Q_UNITS
+            return [(r, sum(sizes[:j]), sizes[j]) for j in range(len(sizes))]
+
+        for r in range(ROUNDS):
+            if r >= 1:
+                for unit in q_units(r - 1):
+                    quantise(*unit)
             if r >= 2:
-                norm_and_store(r - 2)
-            if r < ROUNDS:
-                transpose_and_copy(r)
-            if 1 <= r <= ROUNDS:
-                multiply(r - 1)
+                norm_and_store(r - 2, 0, ROUND)
+            sort_words(r + 1)
+            if r == ROUNDS - 1 and SPLIT_LAST:
+                transpose_and_copy(r, 0, ROUND // 2)
+                multiply(r - 1, 0, ROUND)
+                transpose_and_copy(r, ROUND // 2, ROUND // 2)
+            else:
+                transpose_and_copy(r, 0, ROUND)
+                if r >= 1:
+                    multiply(r - 1, 0, ROUND)
+        last = units(ROUNDS - 1)
+        for j in range(len(last) + 1):
+            if j < len(last):
+                quantise(*last[j])
+                multiply(*last[j])
+            if j == 0:
+                norm_and_store(ROUNDS - 2, 0, ROUND)
+            else:
+                norm_and_store(*last[j - 1])

@@ -30,7 +30,7 @@ V_EXTRA_EVERY = 0
 V_SKIP_EVERY = 0
 TAIL_UNITS = [2, 1, 1]
 Q_UNITS = [4]
-GAIN_BY_PE = False
+GAIN_BY_PE = True
 WARM = 0
 RSQRT = True
 G_GAIN = False

@@ -81,7 +81,6 @@ def tile_combcrossattention_pa_t_kernel(tc, hidden_states, Wq_words, Wq_scales, 
         if GAIN_BY_PE:
             gain_row = const.tile([P, D], BF16)
             nc.vector.memset(gain_row[:], 0.0)
-            nc.scalar.dma_start(out=gain_row[0:1, :], in_=q_norm_w.rearrange("(o d) -> o d", o=1))
         else:
             nc.scalar.dma_start(out=gain[:], in_=q_norm_w.partition_broadcast(P))
         if G_SCALE or G_GAIN:
@@ -100,6 +99,8 @@ def tile_combcrossattention_pa_t_kernel(tc, hidden_states, Wq_words, Wq_scales, 
                 nc.sync.dma_start(out=x_sb[r][:, cols], in_=x_view[r][:, cols])
 
         load_x(0, ROUND)
+        if GAIN_BY_PE:
+            nc.sync.dma_start(out=gain_row[0:1, :], in_=q_norm_w.rearrange("(o d) -> o d", o=1))
         w_words = const.tile([P, PASSES, 2 * N], U8, align_bytes=64)
         nc.sync.dma_start(out=w_words[:].bitcast(I32), in_=Wq_words.rearrange("g p b -> p g b").bitcast(I32))
         for quad in range(4):
@@ -110,7 +111,7 @@ def tile_combcrossattention_pa_t_kernel(tc, hidden_states, Wq_words, Wq_scales, 
         for r in range(1, ROUNDS):
             load_x(r, ROUND if r < FINE_ROUNDS else 1)
 
-        if GAIN_BY_PE:
+        def spread_gain():
             q_ps = q_pool.tile([P, ROUND, N], F32)
             nc.tensor.matmul(q_ps[:, 0, 0:D], lhsT=ones[:], rhs=gain_row[:], start=True, stop=True)
             nc.vector.tensor_copy(out=gain[:], in_=q_ps[:, 0, 0:D])
@@ -294,6 +295,8 @@ def tile_combcrossattention_pa_t_kernel(tc, hidden_states, Wq_words, Wq_scales, 
                 transpose_and_copy(r, ROUND // 2, ROUND // 2)
             else:
                 transpose_and_copy(r, 0, ROUND)
+                if r == 1 and GAIN_BY_PE:
+                    spread_gain()
                 if r >= 1:
                     multiply(r - 1, 0, ROUND)
         last = units(ROUNDS - 1)

@@ -25,6 +25,7 @@ ROUND = 4
 ROUNDS = TILES // ROUND
 HALVES = 2
 FINE_ROUNDS = 3
+W_AFTER = 1
 XT_BANKS = 6
 V_EXTRA_EVERY = 0
 V_SKIP_EVERY = 0
@@ -59,6 +60,10 @@ def tile_combcrossattention_pa_t_kernel(tc, hidden_states, Wq_words, Wq_scales, 
         q_pool = ctx.enter_context(tc.psum_pool(name="q", bufs=2))
         pre_pool = ctx.enter_context(tc.tile_pool(name="pre", bufs=4))
 
+        if GAIN_BY_PE:
+            gain_row = const.tile([P, D], BF16)
+            nc.vector.memset(gain_row[:], 0.0)
+            nc.sync.dma_start(out=gain_row[0:1, :], in_=q_norm_w.rearrange("(o d) -> o d", o=1))
         w_planes = const.tile([P, PASSES, N], U8, align_bytes=64)
         nc.vector.memset(w_planes[:].bitcast(I32), 0)
         eps = const.tile([P, 1], F32)
@@ -78,15 +83,16 @@ def tile_combcrossattention_pa_t_kernel(tc, hidden_states, Wq_words, Wq_scales, 
             for w in range(WARM):
                 xt = xt_pool.tile([P, PASSES * HALVES, P], F32)
                 nc.tensor.matmul(xt[:].rearrange("p a b -> p (a b)"), lhsT=ones[:], rhs=dummy[:], start=True, stop=True)
-        if GAIN_BY_PE:
-            gain_row = const.tile([P, D], BF16)
-            nc.vector.memset(gain_row[:], 0.0)
-        else:
+        if not GAIN_BY_PE:
             nc.scalar.dma_start(out=gain[:], in_=q_norm_w.partition_broadcast(P))
-        if G_SCALE or G_GAIN:
-            gain_all = const.tile([P, ROUND * HEADS, D], BF16)
+        gain_all = const.tile([P, ROUND * HEADS, D], BF16)
+
+        def repeat_gain():
             for c in range(ROUND * HEADS):
                 nc.gpsimd.tensor_copy(out=gain_all[:, c, :], in_=gain[:])
+
+        if (G_SCALE or G_GAIN) and not GAIN_BY_PE:
+            repeat_gain()
         x_sb = []
         for r in range(ROUNDS):
             x_chunk = x_pool.tile([P, ROUND * E], BF16)
@@ -98,29 +104,29 @@ def tile_combcrossattention_pa_t_kernel(tc, hidden_states, Wq_words, Wq_scales, 
                 cols = slice(c * width, (c + 1) * width)
                 nc.sync.dma_start(out=x_sb[r][:, cols], in_=x_view[r][:, cols])
 
-        load_x(0, ROUND)
-        if GAIN_BY_PE:
-            nc.sync.dma_start(out=gain_row[0:1, :], in_=q_norm_w.rearrange("(o d) -> o d", o=1))
         w_words = const.tile([P, PASSES, 2 * N], U8, align_bytes=64)
-        nc.sync.dma_start(out=w_words[:].bitcast(I32), in_=Wq_words.rearrange("g p b -> p g b").bitcast(I32))
-        for quad in range(4):
-            nc.sync.dma_start(
-                out=w_planes[32 * quad : 32 * quad + 4].bitcast(I32),
-                in_=Wq_scales[:, 4 * quad : 4 * quad + 4, :].rearrange("g s n -> s g n").bitcast(I32),
-            )
-        for r in range(1, ROUNDS):
+        for r in range(ROUNDS):
             load_x(r, ROUND if r < FINE_ROUNDS else 1)
+            if r == W_AFTER:
+                nc.sync.dma_start(out=w_words[:].bitcast(I32), in_=Wq_words.rearrange("g p b -> p g b").bitcast(I32))
+                for quad in range(4):
+                    nc.sync.dma_start(
+                        out=w_planes[32 * quad : 32 * quad + 4].bitcast(I32),
+                        in_=Wq_scales[:, 4 * quad : 4 * quad + 4, :].rearrange("g s n -> s g n").bitcast(I32),
+                    )
 
         def spread_gain():
             q_ps = q_pool.tile([P, ROUND, N], F32)
             nc.tensor.matmul(q_ps[:, 0, 0:D], lhsT=ones[:], rhs=gain_row[:], start=True, stop=True)
             nc.vector.tensor_copy(out=gain[:], in_=q_ps[:, 0, 0:D])
+            if G_SCALE or G_GAIN:
+                repeat_gain()
 
         grouped_of, codes_of, scales_of, q_of = {}, {}, {}, {}
         sorted_of = {}
 
         def sort_words(r):
-            if r < PRE_FROM or r >= ROUNDS:
+            if r < PRE_FROM or r >= ROUNDS - G_NOT_LAST:
                 return
             x_words = x_sb[r][:].bitcast(F32)
             for i in PRE_TILES:
@@ -282,6 +288,8 @@ def tile_combcrossattention_pa_t_kernel(tc, hidden_states, Wq_words, Wq_scales, 
             sizes = TAIL_UNITS if r == ROUNDS - 1 else Q_UNITS
             return [(r, sum(sizes[:j]), sizes[j]) for j in range(len(sizes))]
 
+        if GAIN_BY_PE:
+            spread_gain()
         for r in range(ROUNDS):
             if r >= 1:
                 for unit in q_units(r - 1):
@@ -295,8 +303,6 @@ def tile_combcrossattention_pa_t_kernel(tc, hidden_states, Wq_words, Wq_scales, 
                 transpose_and_copy(r, ROUND // 2, ROUND // 2)
             else:
                 transpose_and_copy(r, 0, ROUND)
-                if r == 1 and GAIN_BY_PE:
-                    spread_gain()
                 if r >= 1:
                     multiply(r - 1, 0, ROUND)
         last = units(ROUNDS - 1)

@@ -27,21 +27,7 @@ HALVES = 2
 FINE_ROUNDS = 3
 W_AFTER = 1
 XT_BANKS = 6
-V_EXTRA_EVERY = 0
-V_SKIP_EVERY = 0
 TAIL_UNITS = [2, 1, 1]
-Q_UNITS = [4]
-GAIN_BY_PE = True
-WARM = 0
-RSQRT = True
-G_GAIN = False
-WIDE_SQ = False
-G_PIECES = 1
-G_NOT_LAST = 2
-SPLIT_LAST = False
-G_SCALE = False
-PRE_TILES = ()
-PRE_FROM = 3
 
 FLOPS = 2 * T * E * N
 
@@ -58,41 +44,22 @@ def tile_combcrossattention_pa_t_kernel(tc, hidden_states, Wq_words, Wq_scales, 
         o_pool = ctx.enter_context(tc.tile_pool(name="o", bufs=ROUNDS + len(TAIL_UNITS)))
         xt_pool = ctx.enter_context(tc.psum_pool(name="xt", bufs=XT_BANKS))
         q_pool = ctx.enter_context(tc.psum_pool(name="q", bufs=2))
-        pre_pool = ctx.enter_context(tc.tile_pool(name="pre", bufs=4))
 
-        if GAIN_BY_PE:
-            gain_row = const.tile([P, D], BF16)
-            nc.vector.memset(gain_row[:], 0.0)
-            nc.sync.dma_start(out=gain_row[0:1, :], in_=q_norm_w.rearrange("(o d) -> o d", o=1))
+        gain_row = const.tile([P, D], BF16)
+        nc.vector.memset(gain_row[:], 0.0)
+        nc.sync.dma_start(out=gain_row[0:1, :], in_=q_norm_w.rearrange("(o d) -> o d", o=1))
         w_planes = const.tile([P, PASSES, N], U8, align_bytes=64)
         nc.vector.memset(w_planes[:].bitcast(I32), 0)
         eps = const.tile([P, 1], F32)
         nc.vector.memset(eps[:], EPS)
         warm = const.tile([P, 1], F32)
-        nc.scalar.activation(out=warm[:], in_=eps[:], func=(ACT.Abs_reciprocal_sqrt if RSQRT else ACT.Sqrt))
+        nc.scalar.activation(out=warm[:], in_=eps[:], func=ACT.Abs_reciprocal_sqrt)
         ident = const.tile([P, P], F32)
         make_identity(nc, ident[:])
-
         gain = const.tile([P, D], BF16)
-        if GAIN_BY_PE or WARM:
-            ones = const.tile([P, P], BF16)
-            nc.vector.memset(ones[:], 1.0)
-        if WARM:
-            dummy = const.tile([P, 4 * P], BF16)
-            nc.vector.memset(dummy[:], 0.0)
-            for w in range(WARM):
-                xt = xt_pool.tile([P, PASSES * HALVES, P], F32)
-                nc.tensor.matmul(xt[:].rearrange("p a b -> p (a b)"), lhsT=ones[:], rhs=dummy[:], start=True, stop=True)
-        if not GAIN_BY_PE:
-            nc.scalar.dma_start(out=gain[:], in_=q_norm_w.partition_broadcast(P))
-        gain_all = const.tile([P, ROUND * HEADS, D], BF16)
+        ones = const.tile([P, P], BF16)
+        nc.vector.memset(ones[:], 1.0)
 
-        def repeat_gain():
-            for c in range(ROUND * HEADS):
-                nc.gpsimd.tensor_copy(out=gain_all[:, c, :], in_=gain[:])
-
-        if (G_SCALE or G_GAIN) and not GAIN_BY_PE:
-            repeat_gain()
         x_sb = []
         for r in range(ROUNDS):
             x_chunk = x_pool.tile([P, ROUND * E], BF16)
@@ -116,28 +83,15 @@ def tile_combcrossattention_pa_t_kernel(tc, hidden_states, Wq_words, Wq_scales, 
                     )
 
         def spread_gain():
-            q_ps = q_pool.tile([P, ROUND, N], F32)
-            nc.tensor.matmul(q_ps[:, 0, 0:D], lhsT=ones[:], rhs=gain_row[:], start=True, stop=True)
-            nc.vector.tensor_copy(out=gain[:], in_=q_ps[:, 0, 0:D])
-            if G_SCALE or G_GAIN:
-                repeat_gain()
+            q_bank = q_pool.tile([P, ROUND, N], F32)
+            nc.tensor.matmul(q_bank[:, 0, 0:D], lhsT=ones[:], rhs=gain_row[:], start=True, stop=True)
+            nc.vector.tensor_copy(out=gain[:], in_=q_bank[:, 0, 0:D])
 
         grouped_of, codes_of, scales_of, q_of = {}, {}, {}, {}
-        sorted_of = {}
 
-        def sort_words(r):
-            if r < PRE_FROM or r >= ROUNDS - G_NOT_LAST:
-                return
-            x_words = x_sb[r][:].bitcast(F32)
-            for i in PRE_TILES:
-                x_sorted = pre_pool.tile([P, PASSES, HALVES, P], F32)
-                sorted_of[(r, i)] = x_sorted
-                nc.vector.tensor_copy(
-                    out=x_sorted[:],
-                    in_=x_words[:, i * (E // 2) : (i + 1) * (E // 2)].rearrange("p (g c u) -> p g u c", g=PASSES, u=HALVES),
-                )
+        banks_of = {}
 
-        def transpose_and_copy(r, i0, n):
+        def transpose(r, i0, n):
             x_words = x_sb[r][:].bitcast(F32)
             if i0 == 0:
                 grouped = work.tile([P, ROUND, PASSES, P, 4], BF16, align_bytes=64)
@@ -145,29 +99,22 @@ def tile_combcrossattention_pa_t_kernel(tc, hidden_states, Wq_words, Wq_scales, 
                 codes = work.tile([P, ROUND * PASSES * P], U32, align_bytes=64)
                 x_scales = work.tile([P, ROUND * PASSES * P], U8, align_bytes=64)
                 codes_of[r], scales_of[r] = codes, x_scales
-            grouped = grouped_of[r]
-            banks = {}
             for i in range(i0, i0 + n):
                 xt = xt_pool.tile([P, PASSES * HALVES, P], F32)
-                banks[i] = xt
+                banks_of[(r, i)] = xt
                 for g in range(PASSES):
                     for u in range(HALVES):
                         first = (i * PASSES + g) * (K_PASS // 2)
-                        if (r, i) in sorted_of:
-                            source = sorted_of[(r, i)][:, g, u, :]
-                        else:
-                            source = x_words[:, first + u : first + K_PASS // 2 : HALVES]
+                        source = x_words[:, first + u : first + K_PASS // 2 : HALVES]
                         nc.tensor.transpose(xt[:, g * HALVES + u, :], source, ident[:])
-            v_banks = 2 if (V_EXTRA_EVERY and r % V_EXTRA_EVERY == V_EXTRA_EVERY - 1) else 1
-            if V_SKIP_EVERY and r % V_SKIP_EVERY == V_SKIP_EVERY - 1 and r < ROUNDS - G_NOT_LAST:
-                v_banks = 0
-            for i in range(i0, i0 + n):
-                src = banks[i][:].rearrange("p (g u) c -> p g c u", u=HALVES)
-                dst = grouped[:, i].bitcast(F32)
-                if i % 2 == 0 and i // 2 < v_banks:
-                    nc.vector.tensor_copy(out=dst, in_=src)
-                else:
-                    nc.scalar.copy(out=dst, in_=src)
+
+        def copy_out(r, i):
+            src = banks_of[(r, i)][:].rearrange("p (g u) c -> p g c u", u=HALVES)
+            dst = grouped_of[r][:, i].bitcast(F32)
+            if i == 0:
+                nc.vector.tensor_copy(out=dst, in_=src)
+            else:
+                nc.scalar.copy(out=dst, in_=src)
 
         def quantise(r, i0, n):
             cols = slice(i0 * PASSES * P, (i0 + n) * PASSES * P)
@@ -178,12 +125,15 @@ def tile_combcrossattention_pa_t_kernel(tc, hidden_states, Wq_words, Wq_scales, 
             )
 
         def multiply(r, i0, n):
-            if r == ROUNDS - 1 and len(TAIL_UNITS) > 1:
+            if r == ROUNDS - 1:
                 xt = xt_pool.tile([P, n, N], F32)
-                q_ps = xt
+                q_of[(r, i0)] = xt
+                q_ps = xt[:]
             else:
-                q_ps = q_pool.tile([P, n, N], F32)
-            q_of[(r, i0)] = q_ps
+                if i0 == 0:
+                    q_bank = q_pool.tile([P, ROUND, N], F32)
+                    q_of[(r, 0)] = q_bank
+                q_ps = q_of[(r, 0)][:, i0 : i0 + n, :]
             for i in range(n):
                 for g in range(PASSES):
                     cols = slice(((i0 + i) * PASSES + g) * P, ((i0 + i) * PASSES + g + 1) * P)
@@ -197,28 +147,14 @@ def tile_combcrossattention_pa_t_kernel(tc, hidden_states, Wq_words, Wq_scales, 
                         stop=(g == PASSES - 1),
                     )
 
-        def norm_and_store(r, i0, n):
+        mean_of, rstd_of = {}, {}
+
+        def square(r, i0, n):
             q_ps = q_of[(r, i0)]
-            if G_SCALE:
-                with_gain = work.tile([P, n * HEADS, D], F32)
-                nc.vector.tensor_tensor(
-                    out=with_gain[:],
-                    in0=q_ps[:].rearrange("p i (h d) -> p (i h) d", h=HEADS),
-                    in1=gain_all[:, 0 : n * HEADS, :],
-                    op=ALU.mult,
-                )
             squares = work.tile([P, n * HEADS, D], F32)
             mean_sq = work.tile([P, n * HEADS], F32)
-            wide_sq = WIDE_SQ and r < ROUNDS - G_NOT_LAST
-            if wide_sq:
-                nc.scalar.activation(
-                    out=squares[:].rearrange("p c d -> p (c d)"),
-                    in_=q_ps[:].rearrange("p i n -> p (i n)"),
-                    func=ACT.Square,
-                    scale=D ** -0.5,
-                )
-                nc.vector.tensor_reduce(out=mean_sq[:], in_=squares[:], axis=mybir.AxisListType.X, op=ALU.add)
-            for i in range(0 if wide_sq else n):
+            mean_of[(r, i0)] = mean_sq
+            for i in range(n):
                 for h in range(HEADS):
                     c = i * HEADS + h
                     nc.scalar.activation(
@@ -228,44 +164,18 @@ def tile_combcrossattention_pa_t_kernel(tc, hidden_states, Wq_words, Wq_scales, 
                         scale=D ** -0.5,
                         accum_out=mean_sq[:, c : c + 1],
                     )
+
+        def invert(r, i0, n):
             rstd = work.tile([P, n * HEADS], F32)
-            if RSQRT:
-                nc.scalar.activation(out=rstd[:], in_=mean_sq[:], func=ACT.Abs_reciprocal_sqrt, bias=eps[:, 0:1])
-            else:
-                rms = work.tile([P, n * HEADS], F32)
-                nc.scalar.activation(out=rms[:], in_=mean_sq[:], func=ACT.Sqrt, bias=eps[:, 0:1])
-                nc.vector.reciprocal(out=rstd[:], in_=rms[:])
+            rstd_of[(r, i0)] = rstd
+            nc.scalar.activation(
+                out=rstd[:], in_=mean_of[(r, i0)][:], func=ACT.Abs_reciprocal_sqrt, bias=eps[:, 0:1]
+            )
+
+        def scale_and_store(r, i0, n):
+            q_ps, rstd = q_of[(r, i0)], rstd_of[(r, i0)]
             o_sb = o_pool.tile([P, HEADS, n, D], F32)
-            g_path = G_GAIN and r < ROUNDS - G_NOT_LAST
-            if g_path:
-                by_rms = work.tile([P, HEADS, n, D], F32)
-                nc.vector.tensor_tensor(
-                    out=by_rms[:].rearrange("p h i d -> p i h d"),
-                    in0=q_ps[:].rearrange("p i (h d) -> p i h d", h=HEADS),
-                    in1=rstd[:].rearrange("p (i h) -> p i h", h=HEADS).unsqueeze(3).to_broadcast([P, n, HEADS, D]),
-                    op=ALU.mult,
-                )
-                rows = n * HEADS // min(G_PIECES, n * HEADS)
-                for c in range(0, n * HEADS, rows):
-                    nc.gpsimd.tensor_tensor(
-                        out=o_sb[:].rearrange("p h i d -> p (h i) d")[:, c : c + rows, :],
-                        in0=by_rms[:].rearrange("p h i d -> p (h i) d")[:, c : c + rows, :],
-                        in1=gain_all[:, c : c + rows, :],
-                        op=ALU.mult,
-                    )
-            if G_SCALE:
-                for i in range(n):
-                    for h in range(HEADS):
-                        c = i * HEADS + h
-                        nc.gpsimd.tensor_scalar(
-                            out=o_sb[:, h, i, :],
-                            in0=with_gain[:, c, :],
-                            scalar1=rstd[:, c : c + 1],
-                            scalar2=0.0,
-                            op0=ALU.mult,
-                            op1=ALU.add,
-                        )
-            for i in range(0 if (G_SCALE or g_path) else n):
+            for i in range(n):
                 for h in range(HEADS):
                     c = i * HEADS + h
                     nc.vector.scalar_tensor_tensor(
@@ -280,37 +190,28 @@ def tile_combcrossattention_pa_t_kernel(tc, hidden_states, Wq_words, Wq_scales, 
                 out=out_view[r][:, :, i0 * D : (i0 + n) * D], in_=o_sb[:].rearrange("p h i d -> p h (i d)")
             )
 
-        def units(r):
-            sizes = TAIL_UNITS if r == ROUNDS - 1 else [ROUND]
-            return [(r, sum(sizes[:j]), sizes[j]) for j in range(len(sizes))]
-
-        def q_units(r):
-            sizes = TAIL_UNITS if r == ROUNDS - 1 else Q_UNITS
-            return [(r, sum(sizes[:j]), sizes[j]) for j in range(len(sizes))]
-
-        if GAIN_BY_PE:
-            spread_gain()
-        for r in range(ROUNDS):
-            if r >= 1:
-                for unit in q_units(r - 1):
-                    quantise(*unit)
-            if r >= 2:
-                norm_and_store(r - 2, 0, ROUND)
-            sort_words(r + 1)
-            if r == ROUNDS - 1 and SPLIT_LAST:
-                transpose_and_copy(r, 0, ROUND // 2)
-                multiply(r - 1, 0, ROUND)
-                transpose_and_copy(r, ROUND // 2, ROUND // 2)
-            else:
-                transpose_and_copy(r, 0, ROUND)
+        spread_gain()
+        with tc.manual_schedule(engines={mybir.EngineType.PE, mybir.EngineType.Activation, mybir.EngineType.DVE}):
+            for r in range(ROUNDS):
+                transpose(r, 0, ROUND)
                 if r >= 1:
+                    quantise(r - 1, 0, ROUND)
                     multiply(r - 1, 0, ROUND)
-        last = units(ROUNDS - 1)
+                if r >= 2:
+                    square(r - 2, 0, ROUND)
+                copy_out(r, 0)
+                copy_out(r, 1)
+                if r >= 2:
+                    invert(r - 2, 0, ROUND)
+                    scale_and_store(r - 2, 0, ROUND)
+                copy_out(r, 2)
+                copy_out(r, 3)
+        last = [(ROUNDS - 1, sum(TAIL_UNITS[:j]), TAIL_UNITS[j]) for j in range(len(TAIL_UNITS))]
         for j in range(len(last) + 1):
             if j < len(last):
                 quantise(*last[j])
                 multiply(*last[j])
-            if j == 0:
-                norm_and_store(ROUNDS - 2, 0, ROUND)
-            else:
-                norm_and_store(*last[j - 1])
+            unit = (ROUNDS - 2, 0, ROUND) if j == 0 else last[j - 1]
+            square(*unit)
+            invert(*unit)
+            scale_and_store(*unit)

@@ -44,6 +44,7 @@ def tile_combcrossattention_pa_t_kernel(tc, hidden_states, Wq_words, Wq_scales, 
         o_pool = ctx.enter_context(tc.tile_pool(name="o", bufs=ROUNDS + len(TAIL_UNITS)))
         xt_pool = ctx.enter_context(tc.psum_pool(name="xt", bufs=XT_BANKS))
         q_pool = ctx.enter_context(tc.psum_pool(name="q", bufs=2))
+        sort_pool = ctx.enter_context(tc.tile_pool(name="sorted", bufs=4))
 
         gain_row = const.tile([P, D], BF16)
         nc.vector.memset(gain_row[:], 0.0)
@@ -89,7 +90,17 @@ def tile_combcrossattention_pa_t_kernel(tc, hidden_states, Wq_words, Wq_scales, 
 
         grouped_of, codes_of, scales_of, q_of = {}, {}, {}, {}
 
-        banks_of = {}
+        banks_of, sorted_of = {}, {}
+
+        def sort_words(r, i):
+            x_sorted = sort_pool.tile([P, PASSES, HALVES, P], F32)
+            sorted_of[(r, i)] = x_sorted
+            nc.vector.tensor_copy(
+                out=x_sorted[:],
+                in_=x_sb[r][:].bitcast(F32)[:, i * (E // 2) : (i + 1) * (E // 2)].rearrange(
+                    "p (g c u) -> p g u c", g=PASSES, u=HALVES
+                ),
+            )
 
         def transpose(r, i0, n):
             x_words = x_sb[r][:].bitcast(F32)
@@ -105,7 +116,10 @@ def tile_combcrossattention_pa_t_kernel(tc, hidden_states, Wq_words, Wq_scales, 
                 for g in range(PASSES):
                     for u in range(HALVES):
                         first = (i * PASSES + g) * (K_PASS // 2)
-                        source = x_words[:, first + u : first + K_PASS // 2 : HALVES]
+                        if (r, i) in sorted_of:
+                            source = sorted_of[(r, i)][:, g, u, :]
+                        else:
+                            source = x_words[:, first + u : first + K_PASS // 2 : HALVES]
                         nc.tensor.transpose(xt[:, g * HALVES + u, :], source, ident[:])
 
         def copy_out(r, i):
@@ -204,6 +218,8 @@ def tile_combcrossattention_pa_t_kernel(tc, hidden_states, Wq_words, Wq_scales, 
                 if r >= 2:
                     invert(r - 2, 0, ROUND)
                     scale_and_store(r - 2, 0, ROUND)
+                if r % 2 == 1 and r < ROUNDS - 1:
+                    sort_words(r + 1, ROUND - 1)
                 copy_out(r, 2)
                 copy_out(r, 3)
         last = [(ROUNDS - 1, sum(TAIL_UNITS[:j]), TAIL_UNITS[j]) for j in range(len(TAIL_UNITS))]

@@ -24,7 +24,7 @@ TILES = T // P
 ROUND = 4
 ROUNDS = TILES // ROUND
 HALVES = 2
-FINE_ROUNDS = 3
+FINE_ROUNDS = 5
 W_AFTER = 1
 XT_BANKS = 6
 TAIL_UNITS = [2, 1, 1]

@@ -24,6 +24,7 @@ TILES = T // P
 ROUND = 4
 ROUNDS = TILES // ROUND
 HALVES = 2
+SORT_FROM = 5
 FINE_ROUNDS = 5
 W_AFTER = 1
 XT_BANKS = 6
@@ -91,6 +92,9 @@ def tile_combcrossattention_pa_t_kernel(tc, hidden_states, Wq_words, Wq_scales, 
         grouped_of, codes_of, scales_of, q_of = {}, {}, {}, {}
 
         banks_of, sorted_of = {}, {}
+
+        def is_sorted(r):
+            return SORT_FROM <= r < ROUNDS and r % 3 != 0
 
         def sort_words(r, i):
             x_sorted = sort_pool.tile([P, PASSES, HALVES, P], F32)
@@ -205,11 +209,12 @@ def tile_combcrossattention_pa_t_kernel(tc, hidden_states, Wq_words, Wq_scales, 
             )
 
         spread_gain()
+        half = ROUND // 2
         with tc.manual_schedule(engines={mybir.EngineType.PE, mybir.EngineType.Activation, mybir.EngineType.DVE}):
             for r in range(ROUNDS):
                 transpose(r, 0, ROUND)
                 if r >= 1:
-                    quantise(r - 1, 0, ROUND)
+                    quantise(r - 1, half, half)
                     multiply(r - 1, 0, ROUND)
                 if r >= 2:
                     square(r - 2, 0, ROUND)
@@ -218,8 +223,10 @@ def tile_combcrossattention_pa_t_kernel(tc, hidden_states, Wq_words, Wq_scales, 
                 if r >= 2:
                     invert(r - 2, 0, ROUND)
                     scale_and_store(r - 2, 0, ROUND)
-                if r % 2 == 1 and r < ROUNDS - 1:
+                if is_sorted(r + 1):
                     sort_words(r + 1, ROUND - 1)
+                if r < ROUNDS - 1:
+                    quantise(r, 0, half)
                 copy_out(r, 2)
                 copy_out(r, 3)
         last = [(ROUNDS - 1, sum(TAIL_UNITS[:j]), TAIL_UNITS[j]) for j in range(len(TAIL_UNITS))]

@@ -229,12 +229,16 @@ def tile_combcrossattention_pa_t_kernel(tc, hidden_states, Wq_words, Wq_scales, 
                     quantise(r, 0, half)
                 copy_out(r, 2)
                 copy_out(r, 3)
-        last = [(ROUNDS - 1, sum(TAIL_UNITS[:j]), TAIL_UNITS[j]) for j in range(len(TAIL_UNITS))]
-        for j in range(len(last) + 1):
-            if j < len(last):
-                quantise(*last[j])
-                multiply(*last[j])
-            unit = (ROUNDS - 2, 0, ROUND) if j == 0 else last[j - 1]
-            square(*unit)
-            invert(*unit)
-            scale_and_store(*unit)
+            last = [(ROUNDS - 1, sum(TAIL_UNITS[:j]), TAIL_UNITS[j]) for j in range(len(TAIL_UNITS))]
+            for unit in last:
+                quantise(*unit)
+                multiply(*unit)
+            square(ROUNDS - 2, 0, ROUND)
+            invert(ROUNDS - 2, 0, ROUND)
+            scale_and_store(ROUNDS - 2, 0, ROUND)
+            square(*last[0])
+            for j in range(len(last)):
+                if j + 1 < len(last):
+                    square(*last[j + 1])
+                invert(*last[j])
+                scale_and_store(*last[j])

from contextlib import ExitStack

import concourse.mybir as mybir
from concourse.masks import make_identity

BF16 = mybir.dt.bfloat16
F32 = mybir.dt.float32
I32 = mybir.dt.int32
U8 = mybir.dt.uint8
U32 = mybir.dt.uint32
FP8X4 = mybir.dt.float8_e4m3fn_x4
FP4X4 = mybir.dt.float4_e2m1fn_x4
ACT = mybir.ActivationFunctionType
ALU = mybir.AluOpType

P = 128
T, E = 8192, 1024
HEADS, D = 2, 64
N = HEADS * D
EPS = 1e-05
K_PASS = 4 * P
PASSES = E // K_PASS
TILES = T // P
ROUND = 4
ROUNDS = TILES // ROUND
HALVES = 2
SORT_FROM = 5
FINE_ROUNDS = 5
W_AFTER = 1
XT_BANKS = 6
TAIL_UNITS = [2, 1, 1]

FLOPS = 2 * T * E * N


def tile_combcrossattention_pa_t_kernel(tc, hidden_states, Wq_words, Wq_scales, q_norm_w, out):
    nc = tc.nc
    x_view = hidden_states.rearrange("(r p i) k -> r p (i k)", p=P, i=ROUND)
    out_view = out.rearrange("h (r p i) d -> r p h (i d)", p=P, i=ROUND)

    with ExitStack() as ctx:
        const = ctx.enter_context(tc.tile_pool(name="const", bufs=1))
        x_pool = ctx.enter_context(tc.tile_pool(name="x", bufs=ROUNDS))
        work = ctx.enter_context(tc.tile_pool(name="work", bufs=3))
        o_pool = ctx.enter_context(tc.tile_pool(name="o", bufs=ROUNDS + len(TAIL_UNITS)))
        xt_pool = ctx.enter_context(tc.psum_pool(name="xt", bufs=XT_BANKS))
        q_pool = ctx.enter_context(tc.psum_pool(name="q", bufs=2))
        sort_pool = ctx.enter_context(tc.tile_pool(name="sorted", bufs=4))

        gain_row = const.tile([P, D], BF16)
        nc.vector.memset(gain_row[:], 0.0)
        nc.sync.dma_start(out=gain_row[0:1, :], in_=q_norm_w.rearrange("(o d) -> o d", o=1))
        w_planes = const.tile([P, PASSES, N], U8, align_bytes=64)
        nc.vector.memset(w_planes[:].bitcast(I32), 0)
        eps = const.tile([P, 1], F32)
        nc.vector.memset(eps[:], EPS)
        warm = const.tile([P, 1], F32)
        nc.scalar.activation(out=warm[:], in_=eps[:], func=ACT.Abs_reciprocal_sqrt)
        ident = const.tile([P, P], F32)
        make_identity(nc, ident[:])
        gain = const.tile([P, D], BF16)
        ones = const.tile([P, P], BF16)
        nc.vector.memset(ones[:], 1.0)

        x_sb = []
        for r in range(ROUNDS):
            x_chunk = x_pool.tile([P, ROUND * E], BF16)
            x_sb.append(x_chunk)

        def load_x(r, pieces):
            width = ROUND * E // pieces
            for c in range(pieces):
                cols = slice(c * width, (c + 1) * width)
                nc.sync.dma_start(out=x_sb[r][:, cols], in_=x_view[r][:, cols])

        w_words = const.tile([P, PASSES, 2 * N], U8, align_bytes=64)
        for r in range(ROUNDS):
            load_x(r, ROUND if r < FINE_ROUNDS else 1)
            if r == W_AFTER:
                nc.sync.dma_start(out=w_words[:].bitcast(I32), in_=Wq_words.rearrange("g p b -> p g b").bitcast(I32))
                for quad in range(4):
                    nc.sync.dma_start(
                        out=w_planes[32 * quad : 32 * quad + 4].bitcast(I32),
                        in_=Wq_scales[:, 4 * quad : 4 * quad + 4, :].rearrange("g s n -> s g n").bitcast(I32),
                    )

        def spread_gain():
            q_bank = q_pool.tile([P, ROUND, N], F32)
            nc.tensor.matmul(q_bank[:, 0, 0:D], lhsT=ones[:], rhs=gain_row[:], start=True, stop=True)
            nc.vector.tensor_copy(out=gain[:], in_=q_bank[:, 0, 0:D])

        grouped_of, codes_of, scales_of, q_of = {}, {}, {}, {}

        banks_of, sorted_of = {}, {}

        def is_sorted(r):
            return SORT_FROM <= r < ROUNDS and r % 3 != 0

        def sort_words(r, i):
            x_sorted = sort_pool.tile([P, PASSES, HALVES, P], F32)
            sorted_of[(r, i)] = x_sorted
            nc.vector.tensor_copy(
                out=x_sorted[:],
                in_=x_sb[r][:].bitcast(F32)[:, i * (E // 2) : (i + 1) * (E // 2)].rearrange(
                    "p (g c u) -> p g u c", g=PASSES, u=HALVES
                ),
            )

        def transpose(r, i0, n):
            x_words = x_sb[r][:].bitcast(F32)
            if i0 == 0:
                grouped = work.tile([P, ROUND, PASSES, P, 4], BF16, align_bytes=64)
                grouped_of[r] = grouped
                codes = work.tile([P, ROUND * PASSES * P], U32, align_bytes=64)
                x_scales = work.tile([P, ROUND * PASSES * P], U8, align_bytes=64)
                codes_of[r], scales_of[r] = codes, x_scales
            for i in range(i0, i0 + n):
                xt = xt_pool.tile([P, PASSES * HALVES, P], F32)
                banks_of[(r, i)] = xt
                for g in range(PASSES):
                    for u in range(HALVES):
                        first = (i * PASSES + g) * (K_PASS // 2)
                        if (r, i) in sorted_of:
                            source = sorted_of[(r, i)][:, g, u, :]
                        else:
                            source = x_words[:, first + u : first + K_PASS // 2 : HALVES]
                        nc.tensor.transpose(xt[:, g * HALVES + u, :], source, ident[:])

        def copy_out(r, i):
            src = banks_of[(r, i)][:].rearrange("p (g u) c -> p g c u", u=HALVES)
            dst = grouped_of[r][:, i].bitcast(F32)
            if i == 0:
                nc.vector.tensor_copy(out=dst, in_=src)
            else:
                nc.scalar.copy(out=dst, in_=src)

        def quantise(r, i0, n):
            cols = slice(i0 * PASSES * P, (i0 + n) * PASSES * P)
            nc.vector.quantize_mx(
                out=codes_of[r][:, cols].bitcast(FP8X4),
                scales=scales_of[r][:, cols],
                in_=grouped_of[r][:, i0 : i0 + n].rearrange("p i g c t -> p (i g c t)"),
            )

        def multiply(r, i0, n):
            if r == ROUNDS - 1:
                xt = xt_pool.tile([P, n, N], F32)
                q_of[(r, i0)] = xt
                q_ps = xt[:]
            else:
                if i0 == 0:
                    q_bank = q_pool.tile([P, ROUND, N], F32)
                    q_of[(r, 0)] = q_bank
                q_ps = q_of[(r, 0)][:, i0 : i0 + n, :]
            for i in range(n):
                for g in range(PASSES):
                    cols = slice(((i0 + i) * PASSES + g) * P, ((i0 + i) * PASSES + g + 1) * P)
                    nc.tensor.matmul_mx(
                        out=q_ps[:, i, :],
                        lhsT=codes_of[r][:, cols].bitcast(FP8X4),
                        lhsT_scale=scales_of[r][:, cols],
                        rhs=w_words[:, g, :].bitcast(FP4X4),
                        rhs_scale=w_planes[:, g, :],
                        start=(g == 0),
                        stop=(g == PASSES - 1),
                    )

        mean_of, rstd_of = {}, {}

        def square(r, i0, n):
            q_ps = q_of[(r, i0)]
            squares = work.tile([P, n * HEADS, D], F32)
            mean_sq = work.tile([P, n * HEADS], F32)
            mean_of[(r, i0)] = mean_sq
            for i in range(n):
                for h in range(HEADS):
                    c = i * HEADS + h
                    nc.scalar.activation(
                        out=squares[:, c, :],
                        in_=q_ps[:, i, h * D : (h + 1) * D],
                        func=ACT.Square,
                        scale=D ** -0.5,
                        accum_out=mean_sq[:, c : c + 1],
                    )

        def invert(r, i0, n):
            rstd = work.tile([P, n * HEADS], F32)
            rstd_of[(r, i0)] = rstd
            nc.scalar.activation(
                out=rstd[:], in_=mean_of[(r, i0)][:], func=ACT.Abs_reciprocal_sqrt, bias=eps[:, 0:1]
            )

        def scale_and_store(r, i0, n):
            q_ps, rstd = q_of[(r, i0)], rstd_of[(r, i0)]
            o_sb = o_pool.tile([P, HEADS, n, D], F32)
            for i in range(n):
                for h in range(HEADS):
                    c = i * HEADS + h
                    nc.vector.scalar_tensor_tensor(
                        out=o_sb[:, h, i, :],
                        in0=q_ps[:, i, h * D : (h + 1) * D],
                        scalar=rstd[:, c : c + 1],
                        in1=gain[:],
                        op0=ALU.mult,
                        op1=ALU.mult,
                    )
            nc.sync.dma_start(
                out=out_view[r][:, :, i0 * D : (i0 + n) * D], in_=o_sb[:].rearrange("p h i d -> p h (i d)")
            )

        spread_gain()
        half = ROUND // 2
        with tc.manual_schedule(engines={mybir.EngineType.PE, mybir.EngineType.Activation, mybir.EngineType.DVE}):
            for r in range(ROUNDS):
                transpose(r, 0, ROUND)
                if r >= 1:
                    quantise(r - 1, half, half)
                    multiply(r - 1, 0, ROUND)
                if r >= 2:
                    square(r - 2, 0, ROUND)
                copy_out(r, 0)
                copy_out(r, 1)
                if r >= 2:
                    invert(r - 2, 0, ROUND)
                    scale_and_store(r - 2, 0, ROUND)
                if is_sorted(r + 1):
                    sort_words(r + 1, ROUND - 1)
                if r < ROUNDS - 1:
                    quantise(r, 0, half)
                copy_out(r, 2)
                copy_out(r, 3)
            last = [(ROUNDS - 1, sum(TAIL_UNITS[:j]), TAIL_UNITS[j]) for j in range(len(TAIL_UNITS))]
            for unit in last:
                quantise(*unit)
                multiply(*unit)
            square(ROUNDS - 2, 0, ROUND)
            invert(ROUNDS - 2, 0, ROUND)
            scale_and_store(ROUNDS - 2, 0, ROUND)
            square(*last[0])
            for j in range(len(last)):
                if j + 1 < len(last):
                    square(*last[j + 1])
                invert(*last[j])
                scale_and_store(*last[j])
